import numpy as np
import ml_dtypes

BF16 = ml_dtypes.bfloat16


def bf(x):
    return np.asarray(x, np.float32).astype(BF16)


def f32(x):
    return np.asarray(x, np.float32)


def f64(x):
    return np.asarray(x).astype(np.float64)


def striped(idx):
    return np.tile(idx.reshape(-1, 16).T, (8, 1))


C, K, Q, S, N = 256, 512, 1024, 4096, 1024


def sigmoid(v):
    return 1.0 / (1.0 + np.exp(-v))


def setup_inputs():
    b = 0.1 * np.random.standard_normal((Q, 1))
    b[C:C + C] += 1.0
    return {"base": f32(0.5 * np.random.standard_normal((C, S))), "ctx": bf(np.random.standard_normal((K, N))), "h_prev": bf(np.random.standard_normal((C, N))), "c_prev": f32(np.random.standard_normal((C, N))), "w_x": bf(np.random.standard_normal((K, Q)) / np.sqrt(2.0 * K)), "w_h": bf(np.random.standard_normal((C, Q)) / np.sqrt(2.0 * C)), "b": f32(b), "offs": striped(np.random.permutation(S)[:N])}


def reference(base, ctx, h_prev, c_prev, w_x, w_h, b, offs):
    idx = offs[:16].T.reshape(-1)
    pre = f64(w_x).T @ f64(ctx) + f64(w_h).T @ f64(h_prev) + f64(b)
    a_in, a_keep, a_cand, a_open = pre.reshape(Q // C, C, N)
    c_new = sigmoid(a_keep) * f64(c_prev) + sigmoid(a_in) * np.tanh(a_cand)
    res = f64(base).copy()
    res[:, idx] = sigmoid(a_open) * np.tanh(c_new)
    return res

@@ -1,0 +1,99 @@
+import concourse.mybir as mybir
+
+F32 = mybir.dt.float32
+BF16 = mybir.dt.bfloat16
+U16 = mybir.dt.uint16
+SIGMOID = mybir.ActivationFunctionType.Sigmoid
+TANH = mybir.ActivationFunctionType.Tanh
+MULT = mybir.AluOpType.mult
+
+P = 128
+CHANNELS = 256
+SEQS = 1024
+SLOTS = 4096
+BANK = 512
+PARTS = 4
+CTX_BLOCKS = 4
+HID_BLOCKS = 2
+K_BLOCKS = CTX_BLOCKS + HID_BLOCKS
+CH_BLOCKS = CHANNELS // P
+HALVES = SEQS // BANK
+
+FLOPS = 2 * PARTS * CHANNELS * K_BLOCKS * P * SEQS
+
+
+def tile_improveddecoder_kernel(tc, base, ctx, h_prev, c_prev, w_x, w_h, b, offs, out):
+    nc = tc.nc
+    with (
+        tc.tile_pool(name="held", bufs=1) as held,
+        tc.tile_pool(name="work", bufs=2) as work,
+        tc.psum_pool(name="psum", bufs=2) as psum,
+    ):
+        weights = []
+        moving = []
+        for k in range(K_BLOCKS):
+            w_src, x_src, row = (w_x, ctx, k) if k < CTX_BLOCKS else (w_h, h_prev, k - CTX_BLOCKS)
+            w_tile = held.tile([P, PARTS * CHANNELS], BF16, name=f"weights{k}")
+            x_tile = held.tile([P, SEQS], BF16, name=f"moving{k}")
+            nc.sync.dma_start(w_tile[:], w_src[row * P : (row + 1) * P, :])
+            nc.sync.dma_start(x_tile[:], x_src[row * P : (row + 1) * P, :])
+            weights.append(w_tile)
+            moving.append(x_tile)
+
+        bias = held.tile([P, PARTS * CH_BLOCKS], F32, name="bias")
+        with nc.allow_non_contiguous_dma(reason="4 KiB of bias, one element to a partition"):
+            nc.scalar.dma_start(bias[:], b.rearrange("(t p) o -> p (t o)", p=P))
+
+        offsets = held.tile([P, SEQS // 16], U16, name="offsets")
+        nc.sync.dma_start(offsets[:], offs)
+
+        cell_prev = []
+        window = []
+        for blk in range(CH_BLOCKS):
+            c_tile = held.tile([P, SEQS], F32, name=f"cell_prev{blk}")
+            s_tile = held.tile([P, SLOTS], F32, name=f"window{blk}")
+            nc.sync.dma_start(c_tile[:], c_prev[blk * P : (blk + 1) * P, :])
+            nc.sync.dma_start(s_tile[:], base[blk * P : (blk + 1) * P, :])
+            cell_prev.append(c_tile)
+            window.append(s_tile)
+
+        for blk in range(CH_BLOCKS):
+            open_gate = held.tile([P, SEQS], F32, name=f"open_gate{blk}")
+            tanh_cell = held.tile([P, SEQS], F32, name=f"tanh_cell{blk}")
+            for half in range(HALVES):
+                cols = slice(half * BANK, (half + 1) * BANK)
+                acc = [psum.tile([P, BANK], F32, name=f"acc{part}") for part in range(PARTS)]
+
+                if blk == 0 and half == 0:
+                    steps = [(part, k) for k in range(K_BLOCKS) for part in range(PARTS)]
+                else:
+                    steps = [(part, k) for part in range(PARTS) for k in range(K_BLOCKS)]
+                for part, k in steps:
+                    q0 = part * CHANNELS + blk * P
+                    nc.tensor.matmul(
+                        acc[part][:],
+                        weights[k][:, q0 : q0 + P],
+                        moving[k][:, cols],
+                        start=(k == 0),
+                        stop=(k == K_BLOCKS - 1),
+                    )
+
+                part_bias = [bias[:, part * CH_BLOCKS + blk : part * CH_BLOCKS + blk + 1] for part in range(PARTS)]
+                in_gate = work.tile([P, BANK], F32, name="in_gate")
+                keep_gate = work.tile([P, BANK], F32, name="keep_gate")
+                candidate = work.tile([P, BANK], F32, name="candidate")
+                nc.scalar.activation(in_gate[:], acc[0][:], SIGMOID, bias=part_bias[0])
+                nc.scalar.activation(keep_gate[:], acc[1][:], SIGMOID, bias=part_bias[1])
+                nc.scalar.activation(candidate[:], acc[2][:], TANH, bias=part_bias[2])
+                nc.scalar.activation(open_gate[:, cols], acc[3][:], SIGMOID, bias=part_bias[3])
+
+                kept = work.tile([P, BANK], F32, name="kept")
+                fresh = work.tile([P, BANK], F32, name="fresh")
+                cell = work.tile([P, BANK], F32, name="cell")
+                nc.vector.tensor_mul(kept[:], keep_gate[:], cell_prev[blk][:, cols])
+                nc.vector.tensor_mul(fresh[:], in_gate[:], candidate[:])
+                nc.vector.tensor_add(cell[:], kept[:], fresh[:])
+                nc.scalar.activation(tanh_cell[:, cols], cell[:], TANH)
+
+            nc.vector.tensor_tensor(window[blk][:].indirect(offsets[:]), open_gate[:], tanh_cell[:], MULT)
+            nc.sync.dma_start(out[blk * P : (blk + 1) * P, :], window[blk][:])

@@ -13,6 +13,10 @@ SEQS = 1024
 SLOTS = 4096
 BANK = 512
 PARTS = 4
+IN = 0
+KEEP = 1
+CAND = 2
+OPEN = 3
 CTX_BLOCKS = 4
 HID_BLOCKS = 2
 K_BLOCKS = CTX_BLOCKS + HID_BLOCKS
@@ -58,34 +62,39 @@ def tile_improveddecoder_kernel(tc, base, ctx, h_prev, c_prev, w_x, w_h, b, offs
             window.append(s_tile)
 
         for blk in range(CH_BLOCKS):
+            acc = {
+                (part, half): psum.tile([P, BANK], F32, name=f"acc{part}")
+                for half in range(HALVES)
+                for part in range(PARTS)
+            }
+
+            cell_accs = [(part, half) for half in range(HALVES) for part in (IN, KEEP, CAND)]
+            if blk == 0:
+                steps = [(part, half, k) for k in range(K_BLOCKS) for part, half in cell_accs]
+            else:
+                steps = [(part, half, k) for part, half in cell_accs for k in range(K_BLOCKS)]
+            steps += [(OPEN, half, k) for half in range(HALVES) for k in range(K_BLOCKS)]
+            for part, half, k in steps:
+                q0 = part * CHANNELS + blk * P
+                nc.tensor.matmul(
+                    acc[part, half][:],
+                    weights[k][:, q0 : q0 + P],
+                    moving[k][:, half * BANK : (half + 1) * BANK],
+                    start=(k == 0),
+                    stop=(k == K_BLOCKS - 1),
+                )
+
+            part_bias = [bias[:, part * CH_BLOCKS + blk : part * CH_BLOCKS + blk + 1] for part in range(PARTS)]
             open_gate = held.tile([P, SEQS], F32, name=f"open_gate{blk}")
             tanh_cell = held.tile([P, SEQS], F32, name=f"tanh_cell{blk}")
             for half in range(HALVES):
                 cols = slice(half * BANK, (half + 1) * BANK)
-                acc = [psum.tile([P, BANK], F32, name=f"acc{part}") for part in range(PARTS)]
-
-                if blk == 0 and half == 0:
-                    steps = [(part, k) for k in range(K_BLOCKS) for part in range(PARTS)]
-                else:
-                    steps = [(part, k) for part in range(PARTS) for k in range(K_BLOCKS)]
-                for part, k in steps:
-                    q0 = part * CHANNELS + blk * P
-                    nc.tensor.matmul(
-                        acc[part][:],
-                        weights[k][:, q0 : q0 + P],
-                        moving[k][:, cols],
-                        start=(k == 0),
-                        stop=(k == K_BLOCKS - 1),
-                    )
-
-                part_bias = [bias[:, part * CH_BLOCKS + blk : part * CH_BLOCKS + blk + 1] for part in range(PARTS)]
                 in_gate = work.tile([P, BANK], F32, name="in_gate")
                 keep_gate = work.tile([P, BANK], F32, name="keep_gate")
                 candidate = work.tile([P, BANK], F32, name="candidate")
-                nc.scalar.activation(in_gate[:], acc[0][:], SIGMOID, bias=part_bias[0])
-                nc.scalar.activation(keep_gate[:], acc[1][:], SIGMOID, bias=part_bias[1])
-                nc.scalar.activation(candidate[:], acc[2][:], TANH, bias=part_bias[2])
-                nc.scalar.activation(open_gate[:, cols], acc[3][:], SIGMOID, bias=part_bias[3])
+                nc.scalar.activation(in_gate[:], acc[IN, half][:], SIGMOID, bias=part_bias[IN])
+                nc.scalar.activation(keep_gate[:], acc[KEEP, half][:], SIGMOID, bias=part_bias[KEEP])
+                nc.scalar.activation(candidate[:], acc[CAND, half][:], TANH, bias=part_bias[CAND])
 
                 kept = work.tile([P, BANK], F32, name="kept")
                 fresh = work.tile([P, BANK], F32, name="fresh")
@@ -94,6 +103,9 @@ def tile_improveddecoder_kernel(tc, base, ctx, h_prev, c_prev, w_x, w_h, b, offs
                 nc.vector.tensor_mul(fresh[:], in_gate[:], candidate[:])
                 nc.vector.tensor_add(cell[:], kept[:], fresh[:])
                 nc.scalar.activation(tanh_cell[:, cols], cell[:], TANH)
+            for half in range(HALVES):
+                cols = slice(half * BANK, (half + 1) * BANK)
+                nc.scalar.activation(open_gate[:, cols], acc[OPEN, half][:], SIGMOID, bias=part_bias[OPEN])
 
             nc.vector.tensor_tensor(window[blk][:].indirect(offsets[:]), open_gate[:], tanh_cell[:], MULT)
             nc.sync.dma_start(out[blk * P : (blk + 1) * P, :], window[blk][:])

@@ -12,16 +12,22 @@ CHANNELS = 256
 SEQS = 1024
 SLOTS = 4096
 BANK = 512
+BANKS = 8
+CTX_BLOCKS = 4
+HID_BLOCKS = 2
+K_BLOCKS = CTX_BLOCKS + HID_BLOCKS
+CH_BLOCKS = CHANNELS // P
+
 PARTS = 4
 IN = 0
 KEEP = 1
 CAND = 2
 OPEN = 3
-CTX_BLOCKS = 4
-HID_BLOCKS = 2
-K_BLOCKS = CTX_BLOCKS + HID_BLOCKS
-CH_BLOCKS = CHANNELS // P
-HALVES = SEQS // BANK
+FUNC = {IN: SIGMOID, KEEP: SIGMOID, CAND: TANH, OPEN: SIGMOID}
+
+ORDER = ((IN, 0), (KEEP, 0), (CAND, 0), (IN, 1), (KEEP, 1), (CAND, 1), (OPEN, 0), (OPEN, 1))
+
+FIRST_WAVE = 4
 
 FLOPS = 2 * PARTS * CHANNELS * K_BLOCKS * P * SEQS
 
@@ -31,7 +37,7 @@ def tile_improveddecoder_kernel(tc, base, ctx, h_prev, c_prev, w_x, w_h, b, offs
     with (
         tc.tile_pool(name="held", bufs=1) as held,
         tc.tile_pool(name="work", bufs=2) as work,
-        tc.psum_pool(name="psum", bufs=2) as psum,
+        tc.psum_pool(name="psum", bufs=BANKS) as psum,
     ):
         weights = []
         moving = []
@@ -40,13 +46,13 @@ def tile_improveddecoder_kernel(tc, base, ctx, h_prev, c_prev, w_x, w_h, b, offs
             w_tile = held.tile([P, PARTS * CHANNELS], BF16, name=f"weights{k}")
             x_tile = held.tile([P, SEQS], BF16, name=f"moving{k}")
             nc.sync.dma_start(w_tile[:], w_src[row * P : (row + 1) * P, :])
-            nc.sync.dma_start(x_tile[:], x_src[row * P : (row + 1) * P, :])
+            nc.scalar.dma_start(x_tile[:], x_src[row * P : (row + 1) * P, :])
             weights.append(w_tile)
             moving.append(x_tile)
 
         bias = held.tile([P, PARTS * CH_BLOCKS], F32, name="bias")
         with nc.allow_non_contiguous_dma(reason="4 KiB of bias, one element to a partition"):
-            nc.scalar.dma_start(bias[:], b.rearrange("(t p) o -> p (t o)", p=P))
+            nc.gpsimd.dma_start(bias[:], b.rearrange("(t p) o -> p (t o)", p=P))
 
         offsets = held.tile([P, SEQS // 16], U16, name="offsets")
         nc.sync.dma_start(offsets[:], offs)
@@ -62,50 +68,49 @@ def tile_improveddecoder_kernel(tc, base, ctx, h_prev, c_prev, w_x, w_h, b, offs
             window.append(s_tile)
 
         for blk in range(CH_BLOCKS):
-            acc = {
-                (part, half): psum.tile([P, BANK], F32, name=f"acc{part}")
-                for half in range(HALVES)
-                for part in range(PARTS)
-            }
-
-            cell_accs = [(part, half) for half in range(HALVES) for part in (IN, KEEP, CAND)]
-            if blk == 0:
-                steps = [(part, half, k) for k in range(K_BLOCKS) for part, half in cell_accs]
-            else:
-                steps = [(part, half, k) for part, half in cell_accs for k in range(K_BLOCKS)]
-            steps += [(OPEN, half, k) for half in range(HALVES) for k in range(K_BLOCKS)]
-            for part, half, k in steps:
-                q0 = part * CHANNELS + blk * P
-                nc.tensor.matmul(
-                    acc[part, half][:],
-                    weights[k][:, q0 : q0 + P],
-                    moving[k][:, half * BANK : (half + 1) * BANK],
-                    start=(k == 0),
-                    stop=(k == K_BLOCKS - 1),
-                )
-
-            part_bias = [bias[:, part * CH_BLOCKS + blk : part * CH_BLOCKS + blk + 1] for part in range(PARTS)]
             open_gate = held.tile([P, SEQS], F32, name=f"open_gate{blk}")
             tanh_cell = held.tile([P, SEQS], F32, name=f"tanh_cell{blk}")
-            for half in range(HALVES):
-                cols = slice(half * BANK, (half + 1) * BANK)
-                in_gate = work.tile([P, BANK], F32, name="in_gate")
-                keep_gate = work.tile([P, BANK], F32, name="keep_gate")
-                candidate = work.tile([P, BANK], F32, name="candidate")
-                nc.scalar.activation(in_gate[:], acc[IN, half][:], SIGMOID, bias=part_bias[IN])
-                nc.scalar.activation(keep_gate[:], acc[KEEP, half][:], SIGMOID, bias=part_bias[KEEP])
-                nc.scalar.activation(candidate[:], acc[CAND, half][:], TANH, bias=part_bias[CAND])
+            gate = {}
+            cell_ready = None
 
-                kept = work.tile([P, BANK], F32, name="kept")
-                fresh = work.tile([P, BANK], F32, name="fresh")
-                cell = work.tile([P, BANK], F32, name="cell")
-                nc.vector.tensor_mul(kept[:], keep_gate[:], cell_prev[blk][:, cols])
-                nc.vector.tensor_mul(fresh[:], in_gate[:], candidate[:])
-                nc.vector.tensor_add(cell[:], kept[:], fresh[:])
-                nc.scalar.activation(tanh_cell[:, cols], cell[:], TANH)
-            for half in range(HALVES):
-                cols = slice(half * BANK, (half + 1) * BANK)
-                nc.scalar.activation(open_gate[:, cols], acc[OPEN, half][:], SIGMOID, bias=part_bias[OPEN])
+            first = FIRST_WAVE if blk == 0 else 1
+            waves = [ORDER[:first]] + [ORDER[n : n + 1] for n in range(first, len(ORDER))]
+            for wave in waves:
+                acc = {(part, half): psum.tile([P, BANK], F32, name="acc") for part, half in wave}
+                for k in range(K_BLOCKS):
+                    for part, half in wave:
+                        q0 = part * CHANNELS + blk * P
+                        nc.tensor.matmul(
+                            acc[part, half][:],
+                            weights[k][:, q0 : q0 + P],
+                            moving[k][:, half * BANK : (half + 1) * BANK],
+                            start=(k == 0),
+                            stop=(k == K_BLOCKS - 1),
+                        )
+
+                for part, half in wave:
+                    cols = slice(half * BANK, (half + 1) * BANK)
+                    if part == OPEN:
+                        gate[part] = open_gate[:, cols]
+                    else:
+                        gate[part] = work.tile([P, BANK], F32, name=f"gate{part}")[:]
+                    t = part * CH_BLOCKS + blk
+                    nc.scalar.activation(gate[part], acc[part, half][:], FUNC[part], bias=bias[:, t : t + 1])
+
+                    if cell_ready is not None:
+                        cell, cell_cols = cell_ready
+                        nc.scalar.activation(tanh_cell[:, cell_cols], cell[:], TANH)
+                        cell_ready = None
+
+                    if part == KEEP:
+                        kept = work.tile([P, BANK], F32, name="kept")
+                        nc.vector.tensor_mul(kept[:], gate[KEEP], cell_prev[blk][:, cols])
+                    if part == CAND:
+                        fresh = work.tile([P, BANK], F32, name="fresh")
+                        cell = work.tile([P, BANK], F32, name="cell")
+                        nc.vector.tensor_mul(fresh[:], gate[IN], gate[CAND])
+                        nc.vector.tensor_add(cell[:], kept[:], fresh[:])
+                        cell_ready = (cell, cols)
 
             nc.vector.tensor_tensor(window[blk][:].indirect(offsets[:]), open_gate[:], tanh_cell[:], MULT)
             nc.sync.dma_start(out[blk * P : (blk + 1) * P, :], window[blk][:])

@@ -1,4 +1,5 @@
 import concourse.mybir as mybir
+from concourse.masks import make_identity
 
 F32 = mybir.dt.float32
 BF16 = mybir.dt.bfloat16
@@ -23,6 +24,7 @@ IN = 0
 KEEP = 1
 CAND = 2
 OPEN = 3
+ROW_BLOCKS = PARTS * CH_BLOCKS
 FUNC = {IN: SIGMOID, KEEP: SIGMOID, CAND: TANH, OPEN: SIGMOID}
 
 ORDER = ((IN, 0), (KEEP, 0), (CAND, 0), (IN, 1), (KEEP, 1), (CAND, 1), (OPEN, 0), (OPEN, 1))
@@ -39,6 +41,15 @@ def tile_improveddecoder_kernel(tc, base, ctx, h_prev, c_prev, w_x, w_h, b, offs
         tc.tile_pool(name="work", bufs=2) as work,
         tc.psum_pool(name="psum", bufs=BANKS) as psum,
     ):
+        b_rows = held.tile([ROW_BLOCKS, P], F32, name="b_rows")
+        nc.gpsimd.dma_start(b_rows[:], b.rearrange("(t p) o -> t (p o)", p=P))
+        identity = held.tile([ROW_BLOCKS, ROW_BLOCKS], F32, name="identity")
+        make_identity(nc, identity[:])
+        b_turned = psum.tile([P, ROW_BLOCKS], F32, name="acc")
+        nc.tensor.matmul(b_turned[:], b_rows[:], identity[:], start=True, stop=True)
+        bias = held.tile([P, ROW_BLOCKS], F32, name="bias")
+        nc.vector.tensor_copy(bias[:], b_turned[:])
+
         weights = []
         moving = []
         for k in range(K_BLOCKS):
@@ -49,10 +60,6 @@ def tile_improveddecoder_kernel(tc, base, ctx, h_prev, c_prev, w_x, w_h, b, offs
             nc.scalar.dma_start(x_tile[:], x_src[row * P : (row + 1) * P, :])
             weights.append(w_tile)
             moving.append(x_tile)
-
-        bias = held.tile([P, PARTS * CH_BLOCKS], F32, name="bias")
-        with nc.allow_non_contiguous_dma(reason="4 KiB of bias, one element to a partition"):
-            nc.gpsimd.dma_start(bias[:], b.rearrange("(t p) o -> p (t o)", p=P))
 
         offsets = held.tile([P, SEQS // 16], U16, name="offsets")
         nc.sync.dma_start(offsets[:], offs)

@@ -1,5 +1,4 @@
 import concourse.mybir as mybir
-from concourse.masks import make_identity
 
 F32 = mybir.dt.float32
 BF16 = mybir.dt.bfloat16
@@ -24,12 +23,13 @@ IN = 0
 KEEP = 1
 CAND = 2
 OPEN = 3
-ROW_BLOCKS = PARTS * CH_BLOCKS
 FUNC = {IN: SIGMOID, KEEP: SIGMOID, CAND: TANH, OPEN: SIGMOID}
 
 ORDER = ((IN, 0), (KEEP, 0), (CAND, 0), (IN, 1), (KEEP, 1), (CAND, 1), (OPEN, 0), (OPEN, 1))
 
 FIRST_WAVE = 4
+
+WARM_MATMULS = 6
 
 FLOPS = 2 * PARTS * CHANNELS * K_BLOCKS * P * SEQS
 
@@ -41,14 +41,11 @@ def tile_improveddecoder_kernel(tc, base, ctx, h_prev, c_prev, w_x, w_h, b, offs
         tc.tile_pool(name="work", bufs=2) as work,
         tc.psum_pool(name="psum", bufs=BANKS) as psum,
     ):
-        b_rows = held.tile([ROW_BLOCKS, P], F32, name="b_rows")
-        nc.gpsimd.dma_start(b_rows[:], b.rearrange("(t p) o -> t (p o)", p=P))
-        identity = held.tile([ROW_BLOCKS, ROW_BLOCKS], F32, name="identity")
-        make_identity(nc, identity[:])
-        b_turned = psum.tile([P, ROW_BLOCKS], F32, name="acc")
-        nc.tensor.matmul(b_turned[:], b_rows[:], identity[:], start=True, stop=True)
-        bias = held.tile([P, ROW_BLOCKS], F32, name="bias")
-        nc.vector.tensor_copy(bias[:], b_turned[:])
+        zeros = held.tile([P, BANK], BF16, name="zeros")
+        nc.vector.memset(zeros[:], 0.0)
+        unread = psum.tile([P, BANK], F32, name="acc")
+        for n in range(WARM_MATMULS):
+            nc.tensor.matmul(unread[:], zeros[:, :P], zeros[:], start=True, stop=True)
 
         weights = []
         moving = []
@@ -60,6 +57,10 @@ def tile_improveddecoder_kernel(tc, base, ctx, h_prev, c_prev, w_x, w_h, b, offs
             nc.scalar.dma_start(x_tile[:], x_src[row * P : (row + 1) * P, :])
             weights.append(w_tile)
             moving.append(x_tile)
+
+        bias = held.tile([P, PARTS * CH_BLOCKS], F32, name="bias")
+        with nc.allow_non_contiguous_dma(reason="4 KiB of bias, one element to a partition"):
+            nc.gpsimd.dma_start(bias[:], b.rearrange("(t p) o -> p (t o)", p=P))
 
         offsets = held.tile([P, SEQS // 16], U16, name="offsets")
         nc.sync.dma_start(offsets[:], offs)

@@ -27,7 +27,9 @@ FUNC = {IN: SIGMOID, KEEP: SIGMOID, CAND: TANH, OPEN: SIGMOID}
 
 ORDER = ((IN, 0), (KEEP, 0), (CAND, 0), (IN, 1), (KEEP, 1), (CAND, 1), (OPEN, 0), (OPEN, 1))
 
-FIRST_WAVE = 4
+TANH_AFTER = {(CAND, 1): 0, (OPEN, 0): 1}
+
+FIRST_WAVE = 5
 
 WARM_MATMULS = 6
 
@@ -79,7 +81,7 @@ def tile_improveddecoder_kernel(tc, base, ctx, h_prev, c_prev, w_x, w_h, b, offs
             open_gate = held.tile([P, SEQS], F32, name=f"open_gate{blk}")
             tanh_cell = held.tile([P, SEQS], F32, name=f"tanh_cell{blk}")
             gate = {}
-            cell_ready = None
+            cell = {}
 
             first = FIRST_WAVE if blk == 0 else 1
             waves = [ORDER[:first]] + [ORDER[n : n + 1] for n in range(first, len(ORDER))]
@@ -105,20 +107,18 @@ def tile_improveddecoder_kernel(tc, base, ctx, h_prev, c_prev, w_x, w_h, b, offs
                     t = part * CH_BLOCKS + blk
                     nc.scalar.activation(gate[part], acc[part, half][:], FUNC[part], bias=bias[:, t : t + 1])
 
-                    if cell_ready is not None:
-                        cell, cell_cols = cell_ready
-                        nc.scalar.activation(tanh_cell[:, cell_cols], cell[:], TANH)
-                        cell_ready = None
+                    if (part, half) in TANH_AFTER:
+                        due = TANH_AFTER[part, half]
+                        nc.scalar.activation(tanh_cell[:, due * BANK : (due + 1) * BANK], cell[due][:], TANH)
 
                     if part == KEEP:
                         kept = work.tile([P, BANK], F32, name="kept")
                         nc.vector.tensor_mul(kept[:], gate[KEEP], cell_prev[blk][:, cols])
                     if part == CAND:
                         fresh = work.tile([P, BANK], F32, name="fresh")
-                        cell = work.tile([P, BANK], F32, name="cell")
+                        cell[half] = work.tile([P, BANK], F32, name="cell")
                         nc.vector.tensor_mul(fresh[:], gate[IN], gate[CAND])
-                        nc.vector.tensor_add(cell[:], kept[:], fresh[:])
-                        cell_ready = (cell, cols)
+                        nc.vector.tensor_add(cell[half][:], kept[:], fresh[:])
 
             nc.vector.tensor_tensor(window[blk][:].indirect(offsets[:]), open_gate[:], tanh_cell[:], MULT)
             nc.sync.dma_start(out[blk * P : (blk + 1) * P, :], window[blk][:])

@@ -24,16 +24,16 @@ KEEP = 1
 CAND = 2
 OPEN = 3
 FUNC = {IN: SIGMOID, KEEP: SIGMOID, CAND: TANH, OPEN: SIGMOID}
+PRE_ROWS = PARTS * CHANNELS
+ROW_BLOCKS = PRE_ROWS // P
 
 ORDER = ((IN, 0), (KEEP, 0), (CAND, 0), (IN, 1), (KEEP, 1), (CAND, 1), (OPEN, 0), (OPEN, 1))
 
-TANH_AFTER = {(CAND, 1): 0, (OPEN, 0): 1}
-
 FIRST_WAVE = 5
 
-WARM_MATMULS = 6
+WARM_MATMULS = 4
 
-FLOPS = 2 * PARTS * CHANNELS * K_BLOCKS * P * SEQS
+FLOPS = 2 * PRE_ROWS * K_BLOCKS * P * SEQS
 
 
 def tile_improveddecoder_kernel(tc, base, ctx, h_prev, c_prev, w_x, w_h, b, offs, out):
@@ -53,14 +53,19 @@ def tile_improveddecoder_kernel(tc, base, ctx, h_prev, c_prev, w_x, w_h, b, offs
         moving = []
         for k in range(K_BLOCKS):
             w_src, x_src, row = (w_x, ctx, k) if k < CTX_BLOCKS else (w_h, h_prev, k - CTX_BLOCKS)
-            w_tile = held.tile([P, PARTS * CHANNELS], BF16, name=f"weights{k}")
+            rows = slice(row * P, (row + 1) * P)
+            w_tile = held.tile([P, PRE_ROWS], BF16, name=f"weights{k}")
             x_tile = held.tile([P, SEQS], BF16, name=f"moving{k}")
-            nc.sync.dma_start(w_tile[:], w_src[row * P : (row + 1) * P, :])
-            nc.scalar.dma_start(x_tile[:], x_src[row * P : (row + 1) * P, :])
+            pieces = 2 if k == 0 else 1
+            for n in range(pieces):
+                w_cols = slice(n * PRE_ROWS // pieces, (n + 1) * PRE_ROWS // pieces)
+                x_cols = slice(n * SEQS // pieces, (n + 1) * SEQS // pieces)
+                nc.sync.dma_start(w_tile[:, w_cols], w_src[rows, w_cols])
+                nc.scalar.dma_start(x_tile[:, x_cols], x_src[rows, x_cols])
             weights.append(w_tile)
             moving.append(x_tile)
 
-        bias = held.tile([P, PARTS * CH_BLOCKS], F32, name="bias")
+        bias = held.tile([P, ROW_BLOCKS], F32, name="bias")
         with nc.allow_non_contiguous_dma(reason="4 KiB of bias, one element to a partition"):
             nc.gpsimd.dma_start(bias[:], b.rearrange("(t p) o -> p (t o)", p=P))
 
@@ -81,7 +86,6 @@ def tile_improveddecoder_kernel(tc, base, ctx, h_prev, c_prev, w_x, w_h, b, offs
             open_gate = held.tile([P, SEQS], F32, name=f"open_gate{blk}")
             tanh_cell = held.tile([P, SEQS], F32, name=f"tanh_cell{blk}")
             gate = {}
-            cell = {}
 
             first = FIRST_WAVE if blk == 0 else 1
             waves = [ORDER[:first]] + [ORDER[n : n + 1] for n in range(first, len(ORDER))]
@@ -107,18 +111,15 @@ def tile_improveddecoder_kernel(tc, base, ctx, h_prev, c_prev, w_x, w_h, b, offs
                     t = part * CH_BLOCKS + blk
                     nc.scalar.activation(gate[part], acc[part, half][:], FUNC[part], bias=bias[:, t : t + 1])
 
-                    if (part, half) in TANH_AFTER:
-                        due = TANH_AFTER[part, half]
-                        nc.scalar.activation(tanh_cell[:, due * BANK : (due + 1) * BANK], cell[due][:], TANH)
-
                     if part == KEEP:
                         kept = work.tile([P, BANK], F32, name="kept")
                         nc.vector.tensor_mul(kept[:], gate[KEEP], cell_prev[blk][:, cols])
                     if part == CAND:
                         fresh = work.tile([P, BANK], F32, name="fresh")
-                        cell[half] = work.tile([P, BANK], F32, name="cell")
+                        cell = work.tile([P, BANK], F32, name="cell")
                         nc.vector.tensor_mul(fresh[:], gate[IN], gate[CAND])
-                        nc.vector.tensor_add(cell[half][:], kept[:], fresh[:])
+                        nc.vector.tensor_add(cell[:], kept[:], fresh[:])
+                        nc.scalar.activation(tanh_cell[:, cols], cell[:], TANH)
 
             nc.vector.tensor_tensor(window[blk][:].indirect(offsets[:]), open_gate[:], tanh_cell[:], MULT)
             nc.sync.dma_start(out[blk * P : (blk + 1) * P, :], window[blk][:])

@@ -1,4 +1,5 @@
 import concourse.mybir as mybir
+from concourse.masks import make_identity
 
 F32 = mybir.dt.float32
 BF16 = mybir.dt.bfloat16
@@ -31,7 +32,7 @@ ORDER = ((IN, 0), (KEEP, 0), (CAND, 0), (IN, 1), (KEEP, 1), (CAND, 1), (OPEN, 0)
 
 FIRST_WAVE = 5
 
-WARM_MATMULS = 4
+WARM_MATMULS = 3
 
 FLOPS = 2 * PRE_ROWS * K_BLOCKS * P * SEQS
 
@@ -49,6 +50,15 @@ def tile_improveddecoder_kernel(tc, base, ctx, h_prev, c_prev, w_x, w_h, b, offs
         for n in range(WARM_MATMULS):
             nc.tensor.matmul(unread[:], zeros[:, :P], zeros[:], start=True, stop=True)
 
+        b_rows = held.tile([ROW_BLOCKS, P], F32, name="b_rows")
+        nc.sync.dma_start(b_rows[:], b.rearrange("(t p) o -> t (p o)", p=P))
+        identity = held.tile([ROW_BLOCKS, ROW_BLOCKS], F32, name="identity")
+        make_identity(nc, identity[:])
+        b_turned = psum.tile([P, ROW_BLOCKS], F32, name="acc")
+        nc.tensor.matmul(b_turned[:], b_rows[:], identity[:], start=True, stop=True)
+        bias = held.tile([P, ROW_BLOCKS], F32, name="bias")
+        nc.vector.tensor_copy(bias[:], b_turned[:])
+
         weights = []
         moving = []
         for k in range(K_BLOCKS):
@@ -64,10 +74,6 @@ def tile_improveddecoder_kernel(tc, base, ctx, h_prev, c_prev, w_x, w_h, b, offs
                 nc.scalar.dma_start(x_tile[:, x_cols], x_src[rows, x_cols])
             weights.append(w_tile)
             moving.append(x_tile)
-
-        bias = held.tile([P, ROW_BLOCKS], F32, name="bias")
-        with nc.allow_non_contiguous_dma(reason="4 KiB of bias, one element to a partition"):
-            nc.gpsimd.dma_start(bias[:], b.rearrange("(t p) o -> p (t o)", p=P))
 
         offsets = held.tile([P, SEQS // 16], U16, name="offsets")
         nc.sync.dma_start(offsets[:], offs)

@@ -28,7 +28,8 @@ FUNC = {IN: SIGMOID, KEEP: SIGMOID, CAND: TANH, OPEN: SIGMOID}
 PRE_ROWS = PARTS * CHANNELS
 ROW_BLOCKS = PRE_ROWS // P
 
-ORDER = ((IN, 0), (KEEP, 0), (CAND, 0), (IN, 1), (KEEP, 1), (CAND, 1), (OPEN, 0), (OPEN, 1))
+ORDER = ((IN, 0), (KEEP, 0), (CAND, 0), (OPEN, 0), (IN, 1), (KEEP, 1), (CAND, 1), (OPEN, 1))
+HALF_OFFS = BANK // 16
 
 FIRST_WAVE = 5
 
@@ -127,5 +128,12 @@ def tile_improveddecoder_kernel(tc, base, ctx, h_prev, c_prev, w_x, w_h, b, offs
                         nc.vector.tensor_add(cell[:], kept[:], fresh[:])
                         nc.scalar.activation(tanh_cell[:, cols], cell[:], TANH)
 
-            nc.vector.tensor_tensor(window[blk][:].indirect(offsets[:]), open_gate[:], tanh_cell[:], MULT)
+                    if part == OPEN:
+                        nc.vector.tensor_tensor(
+                            window[blk][:].indirect(offsets[:, half * HALF_OFFS : (half + 1) * HALF_OFFS]),
+                            open_gate[:, cols],
+                            tanh_cell[:, cols],
+                            MULT,
+                        )
+
             nc.sync.dma_start(out[blk * P : (blk + 1) * P, :], window[blk][:])

@@ -18,6 +18,8 @@ CTX_BLOCKS = 4
 HID_BLOCKS = 2
 K_BLOCKS = CTX_BLOCKS + HID_BLOCKS
 CH_BLOCKS = CHANNELS // P
+HALVES = SEQS // BANK
+HALF_OFFS = BANK // 16
 
 PARTS = 4
 IN = 0
@@ -25,13 +27,11 @@ KEEP = 1
 CAND = 2
 OPEN = 3
 FUNC = {IN: SIGMOID, KEEP: SIGMOID, CAND: TANH, OPEN: SIGMOID}
+CELL_PARTS = (IN, KEEP, CAND)
 PRE_ROWS = PARTS * CHANNELS
 ROW_BLOCKS = PRE_ROWS // P
 
-ORDER = ((IN, 0), (KEEP, 0), (CAND, 0), (OPEN, 0), (IN, 1), (KEEP, 1), (CAND, 1), (OPEN, 1))
-HALF_OFFS = BANK // 16
-
-FIRST_WAVE = 5
+UNITS = tuple((blk, half) for half in range(HALVES) for blk in range(CH_BLOCKS))
 
 WARM_MATMULS = 3
 
@@ -60,80 +60,89 @@ def tile_improveddecoder_kernel(tc, base, ctx, h_prev, c_prev, w_x, w_h, b, offs
         bias = held.tile([P, ROW_BLOCKS], F32, name="bias")
         nc.vector.tensor_copy(bias[:], b_turned[:])
 
-        weights = []
-        moving = []
+        weights = [held.tile([P, PRE_ROWS], BF16, name=f"weights{k}") for k in range(K_BLOCKS)]
+        moving = [held.tile([P, K_BLOCKS, BANK], BF16, name=f"moving{half}") for half in range(HALVES)]
+        cell_prev = [held.tile([P, SEQS], F32, name=f"cell_prev{blk}") for blk in range(CH_BLOCKS)]
+        window = [held.tile([P, SLOTS], F32, name=f"window{blk}") for blk in range(CH_BLOCKS)]
+        offsets = held.tile([P, SEQS // 16], U16, name="offsets")
+
+        def load_cell_prev(blk, half):
+            cols = slice(half * BANK, (half + 1) * BANK)
+            nc.sync.dma_start(cell_prev[blk][:, cols], c_prev[blk * P : (blk + 1) * P, cols])
+
+        def load_window(blk):
+            nc.sync.dma_start(window[blk][:], base[blk * P : (blk + 1) * P, :])
+
         for k in range(K_BLOCKS):
             w_src, x_src, row = (w_x, ctx, k) if k < CTX_BLOCKS else (w_h, h_prev, k - CTX_BLOCKS)
             rows = slice(row * P, (row + 1) * P)
-            w_tile = held.tile([P, PRE_ROWS], BF16, name=f"weights{k}")
-            x_tile = held.tile([P, SEQS], BF16, name=f"moving{k}")
             pieces = 2 if k == 0 else 1
             for n in range(pieces):
                 w_cols = slice(n * PRE_ROWS // pieces, (n + 1) * PRE_ROWS // pieces)
-                x_cols = slice(n * SEQS // pieces, (n + 1) * SEQS // pieces)
-                nc.sync.dma_start(w_tile[:, w_cols], w_src[rows, w_cols])
-                nc.scalar.dma_start(x_tile[:, x_cols], x_src[rows, x_cols])
-            weights.append(w_tile)
-            moving.append(x_tile)
+                nc.sync.dma_start(weights[k][:, w_cols], w_src[rows, w_cols])
+            nc.scalar.dma_start(moving[0][:, k, :], x_src[rows, :BANK])
 
-        offsets = held.tile([P, SEQS // 16], U16, name="offsets")
+        load_cell_prev(0, 0)
         nc.sync.dma_start(offsets[:], offs)
+        load_window(0)
+        load_cell_prev(1, 0)
+        nc.sync.dma_start(
+            moving[1][:, :CTX_BLOCKS, :], ctx.rearrange("(k p) j -> p k j", p=P)[:, :, BANK:]
+        )
+        nc.sync.dma_start(
+            moving[1][:, CTX_BLOCKS:, :], h_prev.rearrange("(k p) j -> p k j", p=P)[:, :, BANK:]
+        )
+        load_window(1)
+        load_cell_prev(0, 1)
+        load_cell_prev(1, 1)
 
-        cell_prev = []
-        window = []
-        for blk in range(CH_BLOCKS):
-            c_tile = held.tile([P, SEQS], F32, name=f"cell_prev{blk}")
-            s_tile = held.tile([P, SLOTS], F32, name=f"window{blk}")
-            nc.sync.dma_start(c_tile[:], c_prev[blk * P : (blk + 1) * P, :])
-            nc.sync.dma_start(s_tile[:], base[blk * P : (blk + 1) * P, :])
-            cell_prev.append(c_tile)
-            window.append(s_tile)
+        def accumulate(parts, blk, half):
+            acc = {part: psum.tile([P, BANK], F32, name="acc") for part in parts}
+            for k in range(K_BLOCKS):
+                for part in parts:
+                    q0 = part * CHANNELS + blk * P
+                    nc.tensor.matmul(
+                        acc[part][:],
+                        weights[k][:, q0 : q0 + P],
+                        moving[half][:, k, :],
+                        start=(k == 0),
+                        stop=(k == K_BLOCKS - 1),
+                    )
+            return acc
 
-        for blk in range(CH_BLOCKS):
-            open_gate = held.tile([P, SEQS], F32, name=f"open_gate{blk}")
-            tanh_cell = held.tile([P, SEQS], F32, name=f"tanh_cell{blk}")
+        def gate_of(acc, part, blk):
+            gate = work.tile([P, BANK], F32, name=f"gate{part}")
+            t = part * CH_BLOCKS + blk
+            nc.scalar.activation(gate[:], acc[:], FUNC[part], bias=bias[:, t : t + 1])
+            return gate
+
+        for unit, (blk, half) in enumerate(UNITS):
+            cols = slice(half * BANK, (half + 1) * BANK)
+
             gate = {}
+            groups = [CELL_PARTS] if unit == 0 else [(part,) for part in CELL_PARTS]
+            for parts in groups:
+                acc = accumulate(parts, blk, half)
+                for part in parts:
+                    gate[part] = gate_of(acc[part], part, blk)
 
-            first = FIRST_WAVE if blk == 0 else 1
-            waves = [ORDER[:first]] + [ORDER[n : n + 1] for n in range(first, len(ORDER))]
-            for wave in waves:
-                acc = {(part, half): psum.tile([P, BANK], F32, name="acc") for part, half in wave}
-                for k in range(K_BLOCKS):
-                    for part, half in wave:
-                        q0 = part * CHANNELS + blk * P
-                        nc.tensor.matmul(
-                            acc[part, half][:],
-                            weights[k][:, q0 : q0 + P],
-                            moving[k][:, half * BANK : (half + 1) * BANK],
-                            start=(k == 0),
-                            stop=(k == K_BLOCKS - 1),
-                        )
+            kept = work.tile([P, BANK], F32, name="kept")
+            fresh = work.tile([P, BANK], F32, name="fresh")
+            cell = work.tile([P, BANK], F32, name="cell")
+            nc.vector.tensor_mul(kept[:], gate[KEEP][:], cell_prev[blk][:, cols])
+            nc.vector.tensor_mul(fresh[:], gate[IN][:], gate[CAND][:])
+            nc.vector.tensor_add(cell[:], kept[:], fresh[:])
 
-                for part, half in wave:
-                    cols = slice(half * BANK, (half + 1) * BANK)
-                    if part == OPEN:
-                        gate[part] = open_gate[:, cols]
-                    else:
-                        gate[part] = work.tile([P, BANK], F32, name=f"gate{part}")[:]
-                    t = part * CH_BLOCKS + blk
-                    nc.scalar.activation(gate[part], acc[part, half][:], FUNC[part], bias=bias[:, t : t + 1])
+            acc = accumulate((OPEN,), blk, half)
+            gate[OPEN] = gate_of(acc[OPEN], OPEN, blk)
+            tanh_cell = work.tile([P, BANK], F32, name="tanh_cell")
+            nc.scalar.activation(tanh_cell[:], cell[:], TANH)
 
-                    if part == KEEP:
-                        kept = work.tile([P, BANK], F32, name="kept")
-                        nc.vector.tensor_mul(kept[:], gate[KEEP], cell_prev[blk][:, cols])
-                    if part == CAND:
-                        fresh = work.tile([P, BANK], F32, name="fresh")
-                        cell = work.tile([P, BANK], F32, name="cell")
-                        nc.vector.tensor_mul(fresh[:], gate[IN], gate[CAND])
-                        nc.vector.tensor_add(cell[:], kept[:], fresh[:])
-                        nc.scalar.activation(tanh_cell[:, cols], cell[:], TANH)
-
-                    if part == OPEN:
-                        nc.vector.tensor_tensor(
-                            window[blk][:].indirect(offsets[:, half * HALF_OFFS : (half + 1) * HALF_OFFS]),
-                            open_gate[:, cols],
-                            tanh_cell[:, cols],
-                            MULT,
-                        )
-
-            nc.sync.dma_start(out[blk * P : (blk + 1) * P, :], window[blk][:])
+            nc.vector.tensor_tensor(
+                window[blk][:].indirect(offsets[:, half * HALF_OFFS : (half + 1) * HALF_OFFS]),
+                gate[OPEN][:],
+                tanh_cell[:],
+                MULT,
+            )
+            if half == HALVES - 1:
+                nc.sync.dma_start(out[blk * P : (blk + 1) * P, :], window[blk][:])

@@ -27,11 +27,12 @@ KEEP = 1
 CAND = 2
 OPEN = 3
 FUNC = {IN: SIGMOID, KEEP: SIGMOID, CAND: TANH, OPEN: SIGMOID}
-CELL_PARTS = (IN, KEEP, CAND)
 PRE_ROWS = PARTS * CHANNELS
 ROW_BLOCKS = PRE_ROWS // P
 
-UNITS = tuple((blk, half) for half in range(HALVES) for blk in range(CH_BLOCKS))
+ORDER = ((KEEP, 0), (IN, 0), (CAND, 0), (KEEP, 1), (OPEN, 0), (IN, 1), (CAND, 1), (OPEN, 1))
+
+FIRST_WAVE = 3
 
 WARM_MATMULS = 3
 
@@ -83,9 +84,9 @@ def tile_improveddecoder_kernel(tc, base, ctx, h_prev, c_prev, w_x, w_h, b, offs
             nc.scalar.dma_start(moving[0][:, k, :], x_src[rows, :BANK])
 
         load_cell_prev(0, 0)
+        load_cell_prev(1, 0)
         nc.sync.dma_start(offsets[:], offs)
         load_window(0)
-        load_cell_prev(1, 0)
         nc.sync.dma_start(
             moving[1][:, :CTX_BLOCKS, :], ctx.rearrange("(k p) j -> p k j", p=P)[:, :, BANK:]
         )
@@ -96,13 +97,13 @@ def tile_improveddecoder_kernel(tc, base, ctx, h_prev, c_prev, w_x, w_h, b, offs
         load_cell_prev(0, 1)
         load_cell_prev(1, 1)
 
-        def accumulate(parts, blk, half):
-            acc = {part: psum.tile([P, BANK], F32, name="acc") for part in parts}
+        def accumulate(wave, half):
+            acc = {(part, blk): psum.tile([P, BANK], F32, name="acc") for part, blk in wave}
             for k in range(K_BLOCKS):
-                for part in parts:
+                for part, blk in wave:
                     q0 = part * CHANNELS + blk * P
                     nc.tensor.matmul(
-                        acc[part][:],
+                        acc[part, blk][:],
                         weights[k][:, q0 : q0 + P],
                         moving[half][:, k, :],
                         start=(k == 0),
@@ -116,33 +117,36 @@ def tile_improveddecoder_kernel(tc, base, ctx, h_prev, c_prev, w_x, w_h, b, offs
             nc.scalar.activation(gate[:], acc[:], FUNC[part], bias=bias[:, t : t + 1])
             return gate
 
-        for unit, (blk, half) in enumerate(UNITS):
+        for half in range(HALVES):
             cols = slice(half * BANK, (half + 1) * BANK)
-
             gate = {}
-            groups = [CELL_PARTS] if unit == 0 else [(part,) for part in CELL_PARTS]
-            for parts in groups:
-                acc = accumulate(parts, blk, half)
-                for part in parts:
-                    gate[part] = gate_of(acc[part], part, blk)
+            kept = {}
+            tanh_cell = {}
 
-            kept = work.tile([P, BANK], F32, name="kept")
-            fresh = work.tile([P, BANK], F32, name="fresh")
-            cell = work.tile([P, BANK], F32, name="cell")
-            nc.vector.tensor_mul(kept[:], gate[KEEP][:], cell_prev[blk][:, cols])
-            nc.vector.tensor_mul(fresh[:], gate[IN][:], gate[CAND][:])
-            nc.vector.tensor_add(cell[:], kept[:], fresh[:])
+            first = FIRST_WAVE if half == 0 else 1
+            waves = [ORDER[:first]] + [ORDER[n : n + 1] for n in range(first, len(ORDER))]
+            for wave in waves:
+                acc = accumulate(wave, half)
+                for part, blk in wave:
+                    gate[part, blk] = gate_of(acc[part, blk], part, blk)
 
-            acc = accumulate((OPEN,), blk, half)
-            gate[OPEN] = gate_of(acc[OPEN], OPEN, blk)
-            tanh_cell = work.tile([P, BANK], F32, name="tanh_cell")
-            nc.scalar.activation(tanh_cell[:], cell[:], TANH)
+                    if part == KEEP:
+                        kept[blk] = work.tile([P, BANK], F32, name="kept")
+                        nc.vector.tensor_mul(kept[blk][:], gate[KEEP, blk][:], cell_prev[blk][:, cols])
+                    if part == CAND:
+                        fresh = work.tile([P, BANK], F32, name="fresh")
+                        cell = work.tile([P, BANK], F32, name="cell")
+                        tanh_cell[blk] = work.tile([P, BANK], F32, name="tanh_cell")
+                        nc.vector.tensor_mul(fresh[:], gate[IN, blk][:], gate[CAND, blk][:])
+                        nc.vector.tensor_add(cell[:], kept[blk][:], fresh[:])
+                        nc.scalar.activation(tanh_cell[blk][:], cell[:], TANH)
 
-            nc.vector.tensor_tensor(
-                window[blk][:].indirect(offsets[:, half * HALF_OFFS : (half + 1) * HALF_OFFS]),
-                gate[OPEN][:],
-                tanh_cell[:],
-                MULT,
-            )
-            if half == HALVES - 1:
-                nc.sync.dma_start(out[blk * P : (blk + 1) * P, :], window[blk][:])
+                    if part == OPEN:
+                        nc.vector.tensor_tensor(
+                            window[blk][:].indirect(offsets[:, half * HALF_OFFS : (half + 1) * HALF_OFFS]),
+                            gate[OPEN, blk][:],
+                            tanh_cell[blk][:],
+                            MULT,
+                        )
+                        if half == HALVES - 1:
+                            nc.sync.dma_start(out[blk * P : (blk + 1) * P, :], window[blk][:])

@@ -32,7 +32,7 @@ ROW_BLOCKS = PRE_ROWS // P
 
 ORDER = ((KEEP, 0), (IN, 0), (CAND, 0), (KEEP, 1), (OPEN, 0), (IN, 1), (CAND, 1), (OPEN, 1))
 
-FIRST_WAVE = 3
+FIRST_WAVE = 4
 
 WARM_MATMULS = 3
 

@@ -30,7 +30,22 @@ FUNC = {IN: SIGMOID, KEEP: SIGMOID, CAND: TANH, OPEN: SIGMOID}
 PRE_ROWS = PARTS * CHANNELS
 ROW_BLOCKS = PRE_ROWS // P
 
-ORDER = ((KEEP, 0), (IN, 0), (CAND, 0), (KEEP, 1), (OPEN, 0), (IN, 1), (CAND, 1), (OPEN, 1))
+CELL_PARTS = (KEEP, IN, CAND)
+
+
+def cell_parts(blk, half):
+    return tuple((part, blk, half) for part in CELL_PARTS)
+
+
+ORDER = (
+    cell_parts(0, 0)
+    + cell_parts(1, 0)
+    + ((OPEN, 0, 0),)
+    + cell_parts(0, 1)
+    + ((OPEN, 0, 1), (OPEN, 1, 0))
+    + cell_parts(1, 1)
+    + ((OPEN, 1, 1),)
+)
 
 FIRST_WAVE = 4
 
@@ -43,7 +58,7 @@ def tile_improveddecoder_kernel(tc, base, ctx, h_prev, c_prev, w_x, w_h, b, offs
     nc = tc.nc
     with (
         tc.tile_pool(name="held", bufs=1) as held,
-        tc.tile_pool(name="work", bufs=2) as work,
+        tc.tile_pool(name="work", bufs=3) as work,
         tc.psum_pool(name="psum", bufs=BANKS) as psum,
     ):
         zeros = held.tile([P, BANK], BF16, name="zeros")
@@ -85,25 +100,25 @@ def tile_improveddecoder_kernel(tc, base, ctx, h_prev, c_prev, w_x, w_h, b, offs
 
         load_cell_prev(0, 0)
         load_cell_prev(1, 0)
-        nc.sync.dma_start(offsets[:], offs)
-        load_window(0)
         nc.sync.dma_start(
             moving[1][:, :CTX_BLOCKS, :], ctx.rearrange("(k p) j -> p k j", p=P)[:, :, BANK:]
         )
         nc.sync.dma_start(
             moving[1][:, CTX_BLOCKS:, :], h_prev.rearrange("(k p) j -> p k j", p=P)[:, :, BANK:]
         )
-        load_window(1)
+        nc.sync.dma_start(offsets[:], offs)
+        load_window(0)
         load_cell_prev(0, 1)
         load_cell_prev(1, 1)
+        load_window(1)
 
-        def accumulate(wave, half):
-            acc = {(part, blk): psum.tile([P, BANK], F32, name="acc") for part, blk in wave}
+        def accumulate(wave):
+            acc = {entry: psum.tile([P, BANK], F32, name="acc") for entry in wave}
             for k in range(K_BLOCKS):
-                for part, blk in wave:
+                for part, blk, half in wave:
                     q0 = part * CHANNELS + blk * P
                     nc.tensor.matmul(
-                        acc[part, blk][:],
+                        acc[part, blk, half][:],
                         weights[k][:, q0 : q0 + P],
                         moving[half][:, k, :],
                         start=(k == 0),
@@ -111,42 +126,39 @@ def tile_improveddecoder_kernel(tc, base, ctx, h_prev, c_prev, w_x, w_h, b, offs
                     )
             return acc
 
-        def gate_of(acc, part, blk):
-            gate = work.tile([P, BANK], F32, name=f"gate{part}")
-            t = part * CH_BLOCKS + blk
-            nc.scalar.activation(gate[:], acc[:], FUNC[part], bias=bias[:, t : t + 1])
-            return gate
+        gate = {}
+        kept = {}
+        tanh_cell = {}
 
-        for half in range(HALVES):
-            cols = slice(half * BANK, (half + 1) * BANK)
-            gate = {}
-            kept = {}
-            tanh_cell = {}
+        waves = [ORDER[:FIRST_WAVE]] + [ORDER[n : n + 1] for n in range(FIRST_WAVE, len(ORDER))]
+        for wave in waves:
+            acc = accumulate(wave)
+            for part, blk, half in wave:
+                cols = slice(half * BANK, (half + 1) * BANK)
 
-            first = FIRST_WAVE if half == 0 else 1
-            waves = [ORDER[:first]] + [ORDER[n : n + 1] for n in range(first, len(ORDER))]
-            for wave in waves:
-                acc = accumulate(wave, half)
-                for part, blk in wave:
-                    gate[part, blk] = gate_of(acc[part, blk], part, blk)
+                gate[part, blk, half] = work.tile([P, BANK], F32, name=f"gate{part}")
+                t = part * CH_BLOCKS + blk
+                nc.scalar.activation(
+                    gate[part, blk, half][:], acc[part, blk, half][:], FUNC[part], bias=bias[:, t : t + 1]
+                )
 
-                    if part == KEEP:
-                        kept[blk] = work.tile([P, BANK], F32, name="kept")
-                        nc.vector.tensor_mul(kept[blk][:], gate[KEEP, blk][:], cell_prev[blk][:, cols])
-                    if part == CAND:
-                        fresh = work.tile([P, BANK], F32, name="fresh")
-                        cell = work.tile([P, BANK], F32, name="cell")
-                        tanh_cell[blk] = work.tile([P, BANK], F32, name="tanh_cell")
-                        nc.vector.tensor_mul(fresh[:], gate[IN, blk][:], gate[CAND, blk][:])
-                        nc.vector.tensor_add(cell[:], kept[blk][:], fresh[:])
-                        nc.scalar.activation(tanh_cell[blk][:], cell[:], TANH)
+                if part == KEEP:
+                    kept[blk, half] = work.tile([P, BANK], F32, name="kept")
+                    nc.vector.tensor_mul(kept[blk, half][:], gate[KEEP, blk, half][:], cell_prev[blk][:, cols])
+                if part == CAND:
+                    fresh = work.tile([P, BANK], F32, name="fresh")
+                    cell = work.tile([P, BANK], F32, name="cell")
+                    tanh_cell[blk, half] = work.tile([P, BANK], F32, name="tanh_cell")
+                    nc.vector.tensor_mul(fresh[:], gate[IN, blk, half][:], gate[CAND, blk, half][:])
+                    nc.vector.tensor_add(cell[:], kept[blk, half][:], fresh[:])
+                    nc.scalar.activation(tanh_cell[blk, half][:], cell[:], TANH)
 
-                    if part == OPEN:
-                        nc.vector.tensor_tensor(
-                            window[blk][:].indirect(offsets[:, half * HALF_OFFS : (half + 1) * HALF_OFFS]),
-                            gate[OPEN, blk][:],
-                            tanh_cell[blk][:],
-                            MULT,
-                        )
-                        if half == HALVES - 1:
-                            nc.sync.dma_start(out[blk * P : (blk + 1) * P, :], window[blk][:])
+                if part == OPEN:
+                    nc.vector.tensor_tensor(
+                        window[blk][:].indirect(offsets[:, half * HALF_OFFS : (half + 1) * HALF_OFFS]),
+                        gate[OPEN, blk, half][:],
+                        tanh_cell[blk, half][:],
+                        MULT,
+                    )
+                    if half == HALVES - 1:
+                        nc.sync.dma_start(out[blk * P : (blk + 1) * P, :], window[blk][:])

@@ -49,6 +49,8 @@ ORDER = (
 
 FIRST_WAVE = 4
 
+CHAIN_PIECES = 2
+
 WARM_MATMULS = 3
 
 FLOPS = 2 * PRE_ROWS * K_BLOCKS * P * SEQS
@@ -138,20 +140,27 @@ def tile_improveddecoder_kernel(tc, base, ctx, h_prev, c_prev, w_x, w_h, b, offs
 
                 gate[part, blk, half] = work.tile([P, BANK], F32, name=f"gate{part}")
                 t = part * CH_BLOCKS + blk
-                nc.scalar.activation(
-                    gate[part, blk, half][:], acc[part, blk, half][:], FUNC[part], bias=bias[:, t : t + 1]
-                )
 
-                if part == KEEP:
-                    kept[blk, half] = work.tile([P, BANK], F32, name="kept")
-                    nc.vector.tensor_mul(kept[blk, half][:], gate[KEEP, blk, half][:], cell_prev[blk][:, cols])
                 if part == CAND:
                     fresh = work.tile([P, BANK], F32, name="fresh")
                     cell = work.tile([P, BANK], F32, name="cell")
                     tanh_cell[blk, half] = work.tile([P, BANK], F32, name="tanh_cell")
-                    nc.vector.tensor_mul(fresh[:], gate[IN, blk, half][:], gate[CAND, blk, half][:])
-                    nc.vector.tensor_add(cell[:], kept[blk, half][:], fresh[:])
-                    nc.scalar.activation(tanh_cell[blk, half][:], cell[:], TANH)
+                    for n in range(CHAIN_PIECES):
+                        piece = slice(n * BANK // CHAIN_PIECES, (n + 1) * BANK // CHAIN_PIECES)
+                        nc.scalar.activation(
+                            gate[CAND, blk, half][:, piece], acc[CAND, blk, half][:, piece], TANH, bias=bias[:, t : t + 1]
+                        )
+                        nc.vector.tensor_mul(fresh[:, piece], gate[IN, blk, half][:, piece], gate[CAND, blk, half][:, piece])
+                        nc.vector.tensor_add(cell[:, piece], kept[blk, half][:, piece], fresh[:, piece])
+                        nc.scalar.activation(tanh_cell[blk, half][:, piece], cell[:, piece], TANH)
+                    continue
+
+                nc.scalar.activation(
+                    gate[part, blk, half][:], acc[part, blk, half][:], FUNC[part], bias=bias[:, t : t + 1]
+                )
+                if part == KEEP:
+                    kept[blk, half] = work.tile([P, BANK], F32, name="kept")
+                    nc.vector.tensor_mul(kept[blk, half][:], gate[KEEP, blk, half][:], cell_prev[blk][:, cols])
 
                 if part == OPEN:
                     nc.vector.tensor_tensor(

@@ -94,10 +94,7 @@ def tile_improveddecoder_kernel(tc, base, ctx, h_prev, c_prev, w_x, w_h, b, offs
         for k in range(K_BLOCKS):
             w_src, x_src, row = (w_x, ctx, k) if k < CTX_BLOCKS else (w_h, h_prev, k - CTX_BLOCKS)
             rows = slice(row * P, (row + 1) * P)
-            pieces = 2 if k == 0 else 1
-            for n in range(pieces):
-                w_cols = slice(n * PRE_ROWS // pieces, (n + 1) * PRE_ROWS // pieces)
-                nc.sync.dma_start(weights[k][:, w_cols], w_src[rows, w_cols])
+            nc.sync.dma_start(weights[k][:], w_src[rows, :])
             nc.scalar.dma_start(moving[0][:, k, :], x_src[rows, :BANK])
 
         load_cell_prev(0, 0)

@@ -49,7 +49,8 @@ ORDER = (
 
 FIRST_WAVE = 4
 
-CHAIN_PIECES = 2
+PIECES = 2
+PIECE = BANK // PIECES
 
 WARM_MATMULS = 3
 
@@ -111,18 +112,22 @@ def tile_improveddecoder_kernel(tc, base, ctx, h_prev, c_prev, w_x, w_h, b, offs
         load_cell_prev(1, 1)
         load_window(1)
 
-        def accumulate(wave):
-            acc = {entry: psum.tile([P, BANK], F32, name="acc") for entry in wave}
-            for k in range(K_BLOCKS):
-                for part, blk, half in wave:
-                    q0 = part * CHANNELS + blk * P
-                    nc.tensor.matmul(
-                        acc[part, blk, half][:],
-                        weights[k][:, q0 : q0 + P],
-                        moving[half][:, k, :],
-                        start=(k == 0),
-                        stop=(k == K_BLOCKS - 1),
-                    )
+        def accumulate(wave, pieces):
+            width = BANK // pieces
+            acc = {entry: [] for entry in wave}
+            for n in range(pieces):
+                for entry in wave:
+                    acc[entry].append(psum.tile([P, width], F32, name="acc"))
+                for k in range(K_BLOCKS):
+                    for part, blk, half in wave:
+                        q0 = part * CHANNELS + blk * P
+                        nc.tensor.matmul(
+                            acc[part, blk, half][n][:],
+                            weights[k][:, q0 : q0 + P],
+                            moving[half][:, k, n * width : (n + 1) * width],
+                            start=(k == 0),
+                            stop=(k == K_BLOCKS - 1),
+                        )
             return acc
 
         gate = {}
@@ -131,30 +136,39 @@ def tile_improveddecoder_kernel(tc, base, ctx, h_prev, c_prev, w_x, w_h, b, offs
 
         waves = [ORDER[:FIRST_WAVE]] + [ORDER[n : n + 1] for n in range(FIRST_WAVE, len(ORDER))]
         for wave in waves:
-            acc = accumulate(wave)
+            in_pieces = len(wave) == 1 and wave[0][0] in (CAND, OPEN)
+            acc = accumulate(wave, PIECES if in_pieces else 1)
             for part, blk, half in wave:
                 cols = slice(half * BANK, (half + 1) * BANK)
+                t = part * CH_BLOCKS + blk
+                banks = acc[part, blk, half]
 
                 gate[part, blk, half] = work.tile([P, BANK], F32, name=f"gate{part}")
-                t = part * CH_BLOCKS + blk
+
+                def take(n, pieces):
+                    width = BANK // pieces
+                    first = n * width % (BANK // len(banks))
+                    nc.scalar.activation(
+                        gate[part, blk, half][:, n * width : (n + 1) * width],
+                        banks[n * len(banks) // pieces][:, first : first + width],
+                        FUNC[part],
+                        bias=bias[:, t : t + 1],
+                    )
 
                 if part == CAND:
                     fresh = work.tile([P, BANK], F32, name="fresh")
                     cell = work.tile([P, BANK], F32, name="cell")
                     tanh_cell[blk, half] = work.tile([P, BANK], F32, name="tanh_cell")
-                    for n in range(CHAIN_PIECES):
-                        piece = slice(n * BANK // CHAIN_PIECES, (n + 1) * BANK // CHAIN_PIECES)
-                        nc.scalar.activation(
-                            gate[CAND, blk, half][:, piece], acc[CAND, blk, half][:, piece], TANH, bias=bias[:, t : t + 1]
-                        )
+                    for n in range(PIECES):
+                        piece = slice(n * PIECE, (n + 1) * PIECE)
+                        take(n, PIECES)
                         nc.vector.tensor_mul(fresh[:, piece], gate[IN, blk, half][:, piece], gate[CAND, blk, half][:, piece])
                         nc.vector.tensor_add(cell[:, piece], kept[blk, half][:, piece], fresh[:, piece])
                         nc.scalar.activation(tanh_cell[blk, half][:, piece], cell[:, piece], TANH)
                     continue
 
-                nc.scalar.activation(
-                    gate[part, blk, half][:], acc[part, blk, half][:], FUNC[part], bias=bias[:, t : t + 1]
-                )
+                for n in range(len(banks)):
+                    take(n, len(banks))
                 if part == KEEP:
                     kept[blk, half] = work.tile([P, BANK], F32, name="kept")
                     nc.vector.tensor_mul(kept[blk, half][:], gate[KEEP, blk, half][:], cell_prev[blk][:, cols])

@@ -30,21 +30,23 @@ FUNC = {IN: SIGMOID, KEEP: SIGMOID, CAND: TANH, OPEN: SIGMOID}
 PRE_ROWS = PARTS * CHANNELS
 ROW_BLOCKS = PRE_ROWS // P
 
-CELL_PARTS = (KEEP, IN, CAND)
-
-
-def cell_parts(blk, half):
-    return tuple((part, blk, half) for part in CELL_PARTS)
-
-
 ORDER = (
-    cell_parts(0, 0)
-    + cell_parts(1, 0)
-    + ((OPEN, 0, 0),)
-    + cell_parts(0, 1)
-    + ((OPEN, 0, 1), (OPEN, 1, 0))
-    + cell_parts(1, 1)
-    + ((OPEN, 1, 1),)
+    (KEEP, 0, 0),
+    (IN, 0, 0),
+    (CAND, 0, 0),
+    (KEEP, 1, 0),
+    (IN, 1, 0),
+    (CAND, 1, 0),
+    (OPEN, 0, 0),
+    (KEEP, 1, 1),
+    (IN, 1, 1),
+    (CAND, 1, 1),
+    (OPEN, 1, 0),
+    (OPEN, 1, 1),
+    (KEEP, 0, 1),
+    (IN, 0, 1),
+    (CAND, 0, 1),
+    (OPEN, 0, 1),
 )
 
 FIRST_WAVE = 4
@@ -108,9 +110,9 @@ def tile_improveddecoder_kernel(tc, base, ctx, h_prev, c_prev, w_x, w_h, b, offs
         )
         nc.sync.dma_start(offsets[:], offs)
         load_window(0)
-        load_cell_prev(0, 1)
         load_cell_prev(1, 1)
         load_window(1)
+        load_cell_prev(0, 1)
 
         def accumulate(wave, pieces):
             width = BANK // pieces
@@ -136,7 +138,7 @@ def tile_improveddecoder_kernel(tc, base, ctx, h_prev, c_prev, w_x, w_h, b, offs
 
         waves = [ORDER[:FIRST_WAVE]] + [ORDER[n : n + 1] for n in range(FIRST_WAVE, len(ORDER))]
         for wave in waves:
-            in_pieces = len(wave) == 1 and wave[0][0] in (CAND, OPEN)
+            in_pieces = len(wave) == 1 and wave[0][0] in (OPEN,)
             acc = accumulate(wave, PIECES if in_pieces else 1)
             for part, blk, half in wave:
                 cols = slice(half * BANK, (half + 1) * BANK)
@@ -180,5 +182,5 @@ def tile_improveddecoder_kernel(tc, base, ctx, h_prev, c_prev, w_x, w_h, b, offs
                         tanh_cell[blk, half][:],
                         MULT,
                     )
-                    if half == HALVES - 1:
+                    if (part, blk, half) == [entry for entry in ORDER if entry[:2] == (OPEN, blk)][-1]:
                         nc.sync.dma_start(out[blk * P : (blk + 1) * P, :], window[blk][:])

@@ -52,7 +52,9 @@ ORDER = (
 FIRST_WAVE = 4
 
 PIECES = 2
-PIECE = BANK // PIECES
+
+CHAIN_PIECES = {unit: 1 for unit in ((0, 0), (1, 0), (1, 1))}
+CHAIN_PIECES[ORDER[-1][1:]] = PIECES
 
 WARM_MATMULS = 3
 
@@ -161,9 +163,10 @@ def tile_improveddecoder_kernel(tc, base, ctx, h_prev, c_prev, w_x, w_h, b, offs
                     fresh = work.tile([P, BANK], F32, name="fresh")
                     cell = work.tile([P, BANK], F32, name="cell")
                     tanh_cell[blk, half] = work.tile([P, BANK], F32, name="tanh_cell")
-                    for n in range(PIECES):
-                        piece = slice(n * PIECE, (n + 1) * PIECE)
-                        take(n, PIECES)
+                    width = BANK // CHAIN_PIECES[blk, half]
+                    for n in range(CHAIN_PIECES[blk, half]):
+                        piece = slice(n * width, (n + 1) * width)
+                        take(n, CHAIN_PIECES[blk, half])
                         nc.vector.tensor_mul(fresh[:, piece], gate[IN, blk, half][:, piece], gate[CAND, blk, half][:, piece])
                         nc.vector.tensor_add(cell[:, piece], kept[blk, half][:, piece], fresh[:, piece])
                         nc.scalar.activation(tanh_cell[blk, half][:, piece], cell[:, piece], TANH)

@@ -49,12 +49,16 @@ ORDER = (
     (OPEN, 0, 1),
 )
 
-FIRST_WAVE = 4
+FIRST_WAVE = CH_BLOCKS * 3
+SHARED_K = CTX_BLOCKS
 
 PIECES = 2
 
 CHAIN_PIECES = {unit: 1 for unit in ((0, 0), (1, 0), (1, 1))}
 CHAIN_PIECES[ORDER[-1][1:]] = PIECES
+
+OPEN_PIECES = 4
+SPLIT = ((OPEN, 1, 0), (OPEN, 0, 1))
 
 WARM_MATMULS = 3
 
@@ -122,16 +126,17 @@ def tile_improveddecoder_kernel(tc, base, ctx, h_prev, c_prev, w_x, w_h, b, offs
             for n in range(pieces):
                 for entry in wave:
                     acc[entry].append(psum.tile([P, width], F32, name="acc"))
-                for k in range(K_BLOCKS):
-                    for part, blk, half in wave:
-                        q0 = part * CHANNELS + blk * P
-                        nc.tensor.matmul(
-                            acc[part, blk, half][n][:],
-                            weights[k][:, q0 : q0 + P],
-                            moving[half][:, k, n * width : (n + 1) * width],
-                            start=(k == 0),
-                            stop=(k == K_BLOCKS - 1),
-                        )
+                steps = [(k, entry) for k in range(SHARED_K) for entry in wave]
+                steps += [(k, entry) for entry in wave for k in range(SHARED_K, K_BLOCKS)]
+                for k, (part, blk, half) in steps:
+                    q0 = part * CHANNELS + blk * P
+                    nc.tensor.matmul(
+                        acc[part, blk, half][n][:],
+                        weights[k][:, q0 : q0 + P],
+                        moving[half][:, k, n * width : (n + 1) * width],
+                        start=(k == 0),
+                        stop=(k == K_BLOCKS - 1),
+                    )
             return acc
 
         gate = {}
@@ -140,8 +145,7 @@ def tile_improveddecoder_kernel(tc, base, ctx, h_prev, c_prev, w_x, w_h, b, offs
 
         waves = [ORDER[:FIRST_WAVE]] + [ORDER[n : n + 1] for n in range(FIRST_WAVE, len(ORDER))]
         for wave in waves:
-            in_pieces = len(wave) == 1 and wave[0][0] in (OPEN,)
-            acc = accumulate(wave, PIECES if in_pieces else 1)
+            acc = accumulate(wave, OPEN_PIECES if wave[0] in SPLIT else 1)
             for part, blk, half in wave:
                 cols = slice(half * BANK, (half + 1) * BANK)
                 t = part * CH_BLOCKS + blk

import concourse.mybir as mybir
from concourse.masks import make_identity

F32 = mybir.dt.float32
BF16 = mybir.dt.bfloat16
U16 = mybir.dt.uint16
SIGMOID = mybir.ActivationFunctionType.Sigmoid
TANH = mybir.ActivationFunctionType.Tanh
MULT = mybir.AluOpType.mult

P = 128
CHANNELS = 256
SEQS = 1024
SLOTS = 4096
BANK = 512
BANKS = 8
CTX_BLOCKS = 4
HID_BLOCKS = 2
K_BLOCKS = CTX_BLOCKS + HID_BLOCKS
CH_BLOCKS = CHANNELS // P
HALVES = SEQS // BANK
HALF_OFFS = BANK // 16

PARTS = 4
IN = 0
KEEP = 1
CAND = 2
OPEN = 3
FUNC = {IN: SIGMOID, KEEP: SIGMOID, CAND: TANH, OPEN: SIGMOID}
PRE_ROWS = PARTS * CHANNELS
ROW_BLOCKS = PRE_ROWS // P

ORDER = (
    (KEEP, 0, 0),
    (IN, 0, 0),
    (CAND, 0, 0),
    (KEEP, 1, 0),
    (IN, 1, 0),
    (CAND, 1, 0),
    (OPEN, 0, 0),
    (KEEP, 1, 1),
    (IN, 1, 1),
    (CAND, 1, 1),
    (OPEN, 1, 0),
    (OPEN, 1, 1),
    (KEEP, 0, 1),
    (IN, 0, 1),
    (CAND, 0, 1),
    (OPEN, 0, 1),
)

FIRST_WAVE = CH_BLOCKS * 3
SHARED_K = CTX_BLOCKS

PIECES = 2

CHAIN_PIECES = {unit: 1 for unit in ((0, 0), (1, 0), (1, 1))}
CHAIN_PIECES[ORDER[-1][1:]] = PIECES

OPEN_PIECES = 4
SPLIT = ((OPEN, 1, 0), (OPEN, 0, 1))

WARM_MATMULS = 3

FLOPS = 2 * PRE_ROWS * K_BLOCKS * P * SEQS


def tile_improveddecoder_kernel(tc, base, ctx, h_prev, c_prev, w_x, w_h, b, offs, out):
    nc = tc.nc
    with (
        tc.tile_pool(name="held", bufs=1) as held,
        tc.tile_pool(name="work", bufs=3) as work,
        tc.psum_pool(name="psum", bufs=BANKS) as psum,
    ):
        zeros = held.tile([P, BANK], BF16, name="zeros")
        nc.vector.memset(zeros[:], 0.0)
        unread = psum.tile([P, BANK], F32, name="acc")
        for n in range(WARM_MATMULS):
            nc.tensor.matmul(unread[:], zeros[:, :P], zeros[:], start=True, stop=True)

        b_rows = held.tile([ROW_BLOCKS, P], F32, name="b_rows")
        nc.sync.dma_start(b_rows[:], b.rearrange("(t p) o -> t (p o)", p=P))
        identity = held.tile([ROW_BLOCKS, ROW_BLOCKS], F32, name="identity")
        make_identity(nc, identity[:])
        b_turned = psum.tile([P, ROW_BLOCKS], F32, name="acc")
        nc.tensor.matmul(b_turned[:], b_rows[:], identity[:], start=True, stop=True)
        bias = held.tile([P, ROW_BLOCKS], F32, name="bias")
        nc.vector.tensor_copy(bias[:], b_turned[:])

        weights = [held.tile([P, PRE_ROWS], BF16, name=f"weights{k}") for k in range(K_BLOCKS)]
        moving = [held.tile([P, K_BLOCKS, BANK], BF16, name=f"moving{half}") for half in range(HALVES)]
        cell_prev = [held.tile([P, SEQS], F32, name=f"cell_prev{blk}") for blk in range(CH_BLOCKS)]
        window = [held.tile([P, SLOTS], F32, name=f"window{blk}") for blk in range(CH_BLOCKS)]
        offsets = held.tile([P, SEQS // 16], U16, name="offsets")

        def load_cell_prev(blk, half):
            cols = slice(half * BANK, (half + 1) * BANK)
            nc.sync.dma_start(cell_prev[blk][:, cols], c_prev[blk * P : (blk + 1) * P, cols])

        def load_window(blk):
            nc.sync.dma_start(window[blk][:], base[blk * P : (blk + 1) * P, :])

        for k in range(K_BLOCKS):
            w_src, x_src, row = (w_x, ctx, k) if k < CTX_BLOCKS else (w_h, h_prev, k - CTX_BLOCKS)
            rows = slice(row * P, (row + 1) * P)
            nc.sync.dma_start(weights[k][:], w_src[rows, :])
            nc.scalar.dma_start(moving[0][:, k, :], x_src[rows, :BANK])

        load_cell_prev(0, 0)
        load_cell_prev(1, 0)
        nc.sync.dma_start(
            moving[1][:, :CTX_BLOCKS, :], ctx.rearrange("(k p) j -> p k j", p=P)[:, :, BANK:]
        )
        nc.sync.dma_start(
            moving[1][:, CTX_BLOCKS:, :], h_prev.rearrange("(k p) j -> p k j", p=P)[:, :, BANK:]
        )
        nc.sync.dma_start(offsets[:], offs)
        load_window(0)
        load_cell_prev(1, 1)
        load_window(1)
        load_cell_prev(0, 1)

        def accumulate(wave, pieces):
            width = BANK // pieces
            acc = {entry: [] for entry in wave}
            for n in range(pieces):
                for entry in wave:
                    acc[entry].append(psum.tile([P, width], F32, name="acc"))
                steps = [(k, entry) for k in range(SHARED_K) for entry in wave]
                steps += [(k, entry) for entry in wave for k in range(SHARED_K, K_BLOCKS)]
                for k, (part, blk, half) in steps:
                    q0 = part * CHANNELS + blk * P
                    nc.tensor.matmul(
                        acc[part, blk, half][n][:],
                        weights[k][:, q0 : q0 + P],
                        moving[half][:, k, n * width : (n + 1) * width],
                        start=(k == 0),
                        stop=(k == K_BLOCKS - 1),
                    )
            return acc

        gate = {}
        kept = {}
        tanh_cell = {}

        waves = [ORDER[:FIRST_WAVE]] + [ORDER[n : n + 1] for n in range(FIRST_WAVE, len(ORDER))]
        for wave in waves:
            acc = accumulate(wave, OPEN_PIECES if wave[0] in SPLIT else 1)
            for part, blk, half in wave:
                cols = slice(half * BANK, (half + 1) * BANK)
                t = part * CH_BLOCKS + blk
                banks = acc[part, blk, half]

                gate[part, blk, half] = work.tile([P, BANK], F32, name=f"gate{part}")

                def take(n, pieces):
                    width = BANK // pieces
                    first = n * width % (BANK // len(banks))
                    nc.scalar.activation(
                        gate[part, blk, half][:, n * width : (n + 1) * width],
                        banks[n * len(banks) // pieces][:, first : first + width],
                        FUNC[part],
                        bias=bias[:, t : t + 1],
                    )

                if part == CAND:
                    fresh = work.tile([P, BANK], F32, name="fresh")
                    cell = work.tile([P, BANK], F32, name="cell")
                    tanh_cell[blk, half] = work.tile([P, BANK], F32, name="tanh_cell")
                    width = BANK // CHAIN_PIECES[blk, half]
                    for n in range(CHAIN_PIECES[blk, half]):
                        piece = slice(n * width, (n + 1) * width)
                        take(n, CHAIN_PIECES[blk, half])
                        nc.vector.tensor_mul(fresh[:, piece], gate[IN, blk, half][:, piece], gate[CAND, blk, half][:, piece])
                        nc.vector.tensor_add(cell[:, piece], kept[blk, half][:, piece], fresh[:, piece])
                        nc.scalar.activation(tanh_cell[blk, half][:, piece], cell[:, piece], TANH)
                    continue

                for n in range(len(banks)):
                    take(n, len(banks))
                if part == KEEP:
                    kept[blk, half] = work.tile([P, BANK], F32, name="kept")
                    nc.vector.tensor_mul(kept[blk, half][:], gate[KEEP, blk, half][:], cell_prev[blk][:, cols])

                if part == OPEN:
                    nc.vector.tensor_tensor(
                        window[blk][:].indirect(offsets[:, half * HALF_OFFS : (half + 1) * HALF_OFFS]),
                        gate[OPEN, blk, half][:],
                        tanh_cell[blk, half][:],
                        MULT,
                    )
                    if (part, blk, half) == [entry for entry in ORDER if entry[:2] == (OPEN, blk)][-1]:
                        nc.sync.dma_start(out[blk * P : (blk + 1) * P, :], window[blk][:])
